import numpy as np
import ml_dtypes


def mxq(x, axis, fmt="e4m3"):
    dtype, down = {"e4m3": (ml_dtypes.float8_e4m3fn, 7), "e5m2": (ml_dtypes.float8_e5m2, 14)}[fmt]
    v = np.moveaxis(np.asarray(x, np.float32).astype(ml_dtypes.bfloat16).astype(np.float64), axis, -1)
    blocks = v.reshape(v.shape[:-1] + (-1, 32))
    amax = np.abs(blocks).max(-1, keepdims=True)
    byte = np.maximum(np.where(amax > 0, np.frexp(amax)[1] - 1 + 127, 0) - down, 1)
    scale = np.exp2(byte - 127.0)
    codes = (blocks / scale).astype(np.float32).astype(dtype).astype(np.float64)
    return np.moveaxis((codes * scale).reshape(v.shape), -1, axis)


WIDE = False


def mx_kscale(k):
    if not WIDE:
        return np.ones(k)
    levels = np.array([10, -10, 5, -5, 0])
    if k % 512:
        return np.exp2(np.random.permutation(np.resize(levels, k // 32))).repeat(32)
    a = np.empty((k // 512, 16))
    for p in range(k // 512):
        a[p, :8] = np.random.permutation(np.resize(levels, 8))
        for g in range(8):
            far = levels[np.abs(levels - a[p, g]) >= 10]
            a[p, g + 8] = far[np.random.randint(len(far))]
    return np.exp2(a.ravel()).repeat(32)


BF16 = ml_dtypes.bfloat16


def bf(x):
    return np.asarray(x, np.float32).astype(BF16)


def f64(x):
    return np.asarray(x).astype(np.float64)


T, D, E = 4096, 512, 1024


def setup_inputs():
    s = mx_kscale(D)
    return {"hidden_states": bf(np.random.standard_normal((T, D)) * s),
            "weight": bf(np.random.standard_normal((E, D)) * 1.0 / np.sqrt(D) / s[None, :])}


def reference(hidden_states, weight):
    logits = mxq(f64(hidden_states), 1, "e4m3") @ mxq(f64(weight), 1, "e4m3").T
    return logits

@@ -1,0 +1,146 @@
+from contextlib import ExitStack
+
+import concourse.mybir as mybir
+from concourse.masks import make_identity
+
+F32 = mybir.dt.float32
+BF16 = mybir.dt.bfloat16
+U32 = mybir.dt.uint32
+U8 = mybir.dt.uint8
+FP8X4 = mybir.dt.float8_e4m3fn_x4
+
+T, D, E = 4096, 512, 1024
+P = 128
+SLOTS = T // P
+PAIRS = SLOTS // 2
+HALF = 512
+FLOPS = 2 * T * D * E
+
+LOAD_SLOTS = (2, 2, 4, 8, 8, 8)
+STORE_SLOTS = (1, 1, 2, 2, 2, 2, 2, 4, 4, 4, 4, 2, 1, 1)
+
+
+def tile_longcatrouter_t_kernel(tc, hidden_states, weight, out):
+    nc = tc.nc
+    x_view = hidden_states.rearrange("(p s) d -> p s d", s=SLOTS)
+    o_view = out.rearrange("(p s) e -> p s e", s=SLOTS)
+    w_view = weight.rearrange("(b p a) d -> p b a d", b=4, a=2)
+
+    with ExitStack() as ctx:
+        keep = ctx.enter_context(tc.tile_pool(name="keep", bufs=1))
+        stage = ctx.enter_context(tc.tile_pool(name="stage", bufs=4))
+        psum = ctx.enter_context(tc.psum_pool(name="psum", bufs=8))
+        ctx.enter_context(tc.manual_schedule())
+
+        ident = keep.tile([P, P], F32, name="ident")
+        make_identity(nc, ident[:])
+
+        x_rows = []
+        w_rows = []
+
+        def load_x(c):
+            n = LOAD_SLOTS[c]
+            first = sum(LOAD_SLOTS[:c])
+            xt = keep.tile([P, n, D], BF16, name="x%d" % c)
+            nc.sync.dma_start(out=xt[:], in_=x_view[:, first : first + n, :])
+            for j in range(n):
+                x_rows.append(xt[:, j, :])
+
+        load_x(0)
+        for h in range(2):
+            wt = keep.tile([P, 2, 2, D], BF16, name="w%d" % h)
+            nc.sync.dma_start(out=wt[:], in_=w_view[:, 2 * h : 2 * h + 2, :, :])
+            for i in range(2):
+                for a in range(2):
+                    w_rows.append(wt[:, i, a, :])
+        for c in range(1, len(LOAD_SLOTS)):
+            load_x(c)
+
+        def gather(rows, order):
+            bank = psum.tile([P, 4 * P], F32, name="tp", tag="bank")
+            for a in range(2):
+                words = rows[a].bitcast(F32)
+                for u in range(2):
+                    q = 2 * a + u
+                    nc.tensor.transpose(
+                        bank[:, q * P : (q + 1) * P], words[:, u::2], ident[:]
+                    )
+            grouped = stage.tile([P, 8 * P], BF16, name="grouped", align_bytes=64)
+            nc.scalar.copy(
+                out=grouped[:].bitcast(F32).rearrange("p (%s) -> p %s" % (order, order), a=2, u=2),
+                in_=bank[:].rearrange("p (a u c) -> p %s" % order, a=2, u=2),
+            )
+            return grouped
+
+        def quantise(grouped, codes, scales):
+            nc.vector.quantize_mx(out=codes.bitcast(FP8X4), scales=scales, in_=grouped[:])
+
+        x_grouped = {}
+        x_codes = {}
+        x_scales = {}
+
+        def gather_x(g):
+            x_grouped[g] = gather(x_rows[2 * g : 2 * g + 2], "a c u")
+
+        def quantise_x(g):
+            x_codes[g] = keep.tile([P, 2 * P], U32, name="xc%d" % g, align_bytes=64)
+            x_scales[g] = keep.tile([P, 2 * P], U8, name="xs%d" % g, align_bytes=64)
+            quantise(x_grouped[g], x_codes[g][:], x_scales[g][:])
+
+        store_of = {}
+        first = 0
+        for c, n in enumerate(STORE_SLOTS):
+            ot = keep.tile([P, n, E], F32, name="o%d" % c)
+            for j in range(n):
+                store_of[first + j] = (ot, j, first, n)
+            first += n
+
+        w_codes = []
+        w_scales = []
+
+        def multiply(g):
+            for h in range(2):
+                for a in range(2):
+                    ot, j, first, n = store_of[2 * g + a]
+                    cols = slice(a * P, (a + 1) * P)
+                    acc = psum.tile([P, HALF], F32, name="acc", tag="bank")
+                    nc.tensor.matmul_mx(
+                        out=acc[:],
+                        lhsT=x_codes[g][:, cols].bitcast(FP8X4),
+                        lhsT_scale=x_scales[g][:, cols],
+                        rhs=w_codes[h][:].bitcast(FP8X4),
+                        rhs_scale=w_scales[h][:],
+                        start=True,
+                        stop=True,
+                    )
+                    dst = ot[:, j, h * HALF : (h + 1) * HALF]
+                    if a == 0 or (h == 1 and g % 3 == 2):
+                        nc.vector.tensor_copy(out=dst, in_=acc[:])
+                    else:
+                        nc.scalar.copy(out=dst, in_=acc[:])
+            for a in range(2):
+                ot, j, first, n = store_of[2 * g + a]
+                if j == n - 1:
+                    nc.sync.dma_start(out=o_view[:, first : first + n, :], in_=ot[:])
+
+        gather_x(0)
+        quantise_x(0)
+        for h in range(2):
+            wc = keep.tile([P, HALF], U32, name="wc%d" % h, align_bytes=64)
+            ws = keep.tile([P, HALF], U8, name="ws%d" % h, align_bytes=64)
+            for i in range(2):
+                b = 2 * h + i
+                cols = slice(2 * P * i, 2 * P * (i + 1))
+                quantise(gather(w_rows[2 * b : 2 * b + 2], "c a u"), wc[:, cols], ws[:, cols])
+            w_codes.append(wc)
+            w_scales.append(ws)
+
+        rounds = [[0], [1]] + [[g, g + 1] for g in range(2, PAIRS, 2)] + [[]]
+        for k in range(len(rounds) - 1):
+            for g in rounds[k + 1]:
+                gather_x(g)
+            for i, g in enumerate(rounds[k]):
+                multiply(g)
+                if i == 0:
+                    for q in rounds[k + 1]:
+                        quantise_x(q)

@@ -17,7 +17,7 @@ HALF = 512
 FLOPS = 2 * T * D * E
 
 LOAD_SLOTS = (2, 2, 4, 8, 8, 8)
-STORE_SLOTS = (1, 1, 2, 2, 2, 2, 2, 4, 4, 4, 4, 2, 1, 1)
+STORE_SLOTS = (2, 2, 2, 2, 4, 4, 8, 8)
 
 
 def tile_longcatrouter_t_kernel(tc, hidden_states, weight, out):

@@ -16,7 +16,7 @@ PAIRS = SLOTS // 2
 HALF = 512
 FLOPS = 2 * T * D * E
 
-LOAD_SLOTS = (2, 2, 4, 8, 8, 8)
+LOAD_SLOTS = (2, 6, 8, 16)
 STORE_SLOTS = (2, 2, 2, 2, 4, 4, 8, 8)
 
 
@@ -24,7 +24,7 @@ def tile_longcatrouter_t_kernel(tc, hidden_states, weight, out):
     nc = tc.nc
     x_view = hidden_states.rearrange("(p s) d -> p s d", s=SLOTS)
     o_view = out.rearrange("(p s) e -> p s e", s=SLOTS)
-    w_view = weight.rearrange("(b p a) d -> p b a d", b=4, a=2)
+    w_view = weight.rearrange("(h p j) d -> p h j d", h=2, j=4)
 
     with ExitStack() as ctx:
         keep = ctx.enter_context(tc.tile_pool(name="keep", bufs=1))
@@ -48,15 +48,14 @@ def tile_longcatrouter_t_kernel(tc, hidden_states, weight, out):
 
         load_x(0)
         for h in range(2):
-            wt = keep.tile([P, 2, 2, D], BF16, name="w%d" % h)
-            nc.sync.dma_start(out=wt[:], in_=w_view[:, 2 * h : 2 * h + 2, :, :])
-            for i in range(2):
-                for a in range(2):
-                    w_rows.append(wt[:, i, a, :])
+            wt = keep.tile([P, 4, D], BF16, name="w%d" % h)
+            nc.sync.dma_start(out=wt[:], in_=w_view[:, h, :, :])
+            for j in range(4):
+                w_rows.append(wt[:, j, :])
         for c in range(1, len(LOAD_SLOTS)):
             load_x(c)
 
-        def gather(rows, order):
+        def transpose_pair(rows):
             bank = psum.tile([P, 4 * P], F32, name="tp", tag="bank")
             for a in range(2):
                 words = rows[a].bitcast(F32)
@@ -65,12 +64,7 @@ def tile_longcatrouter_t_kernel(tc, hidden_states, weight, out):
                     nc.tensor.transpose(
                         bank[:, q * P : (q + 1) * P], words[:, u::2], ident[:]
                     )
-            grouped = stage.tile([P, 8 * P], BF16, name="grouped", align_bytes=64)
-            nc.scalar.copy(
-                out=grouped[:].bitcast(F32).rearrange("p (%s) -> p %s" % (order, order), a=2, u=2),
-                in_=bank[:].rearrange("p (a u c) -> p %s" % order, a=2, u=2),
-            )
-            return grouped
+            return bank
 
         def quantise(grouped, codes, scales):
             nc.vector.quantize_mx(out=codes.bitcast(FP8X4), scales=scales, in_=grouped[:])
@@ -80,7 +74,13 @@ def tile_longcatrouter_t_kernel(tc, hidden_states, weight, out):
         x_scales = {}
 
         def gather_x(g):
-            x_grouped[g] = gather(x_rows[2 * g : 2 * g + 2], "a c u")
+            bank = transpose_pair(x_rows[2 * g : 2 * g + 2])
+            grouped = stage.tile([P, 8 * P], BF16, name="grouped", align_bytes=64)
+            nc.scalar.copy(
+                out=grouped[:].bitcast(F32).rearrange("p (a c u) -> p a c u", a=2, u=2),
+                in_=bank[:].rearrange("p (a u c) -> p a c u", a=2, u=2),
+            )
+            x_grouped[g] = grouped
 
         def quantise_x(g):
             x_codes[g] = keep.tile([P, 2 * P], U32, name="xc%d" % g, align_bytes=64)
@@ -128,10 +128,13 @@ def tile_longcatrouter_t_kernel(tc, hidden_states, weight, out):
         for h in range(2):
             wc = keep.tile([P, HALF], U32, name="wc%d" % h, align_bytes=64)
             ws = keep.tile([P, HALF], U8, name="ws%d" % h, align_bytes=64)
-            for i in range(2):
-                b = 2 * h + i
-                cols = slice(2 * P * i, 2 * P * (i + 1))
-                quantise(gather(w_rows[2 * b : 2 * b + 2], "c a u"), wc[:, cols], ws[:, cols])
+            grouped = keep.tile([P, 4 * HALF], BF16, name="wg%d" % h, align_bytes=64)
+            words = grouped[:].bitcast(F32).rearrange("p (c b x) -> p b c x", b=2, x=4)
+            for b in range(2):
+                bank = transpose_pair(w_rows[4 * h + 2 * b : 4 * h + 2 * b + 2])
+                copy = nc.scalar.copy if b == 0 else nc.vector.tensor_copy
+                copy(out=words[:, b], in_=bank[:].rearrange("p (x c) -> p c x", x=4))
+            quantise(grouped, wc[:], ws[:])
             w_codes.append(wc)
             w_scales.append(ws)
 

from contextlib import ExitStack

import concourse.mybir as mybir
from concourse.masks import make_identity

F32 = mybir.dt.float32
BF16 = mybir.dt.bfloat16
U32 = mybir.dt.uint32
U8 = mybir.dt.uint8
FP8X4 = mybir.dt.float8_e4m3fn_x4

T, D, E = 4096, 512, 1024
P = 128
SLOTS = T // P
PAIRS = SLOTS // 2
HALF = 512
FLOPS = 2 * T * D * E

LOAD_SLOTS = (2, 6, 8, 16)
STORE_SLOTS = (2, 2, 2, 2, 4, 4, 8, 8)


def tile_longcatrouter_t_kernel(tc, hidden_states, weight, out):
    nc = tc.nc
    x_view = hidden_states.rearrange("(p s) d -> p s d", s=SLOTS)
    o_view = out.rearrange("(p s) e -> p s e", s=SLOTS)
    w_view = weight.rearrange("(h p j) d -> p h j d", h=2, j=4)

    with ExitStack() as ctx:
        keep = ctx.enter_context(tc.tile_pool(name="keep", bufs=1))
        stage = ctx.enter_context(tc.tile_pool(name="stage", bufs=4))
        psum = ctx.enter_context(tc.psum_pool(name="psum", bufs=8))
        ctx.enter_context(tc.manual_schedule())

        ident = keep.tile([P, P], F32, name="ident")
        make_identity(nc, ident[:])

        x_rows = []
        w_rows = []

        def load_x(c):
            n = LOAD_SLOTS[c]
            first = sum(LOAD_SLOTS[:c])
            xt = keep.tile([P, n, D], BF16, name="x%d" % c)
            nc.sync.dma_start(out=xt[:], in_=x_view[:, first : first + n, :])
            for j in range(n):
                x_rows.append(xt[:, j, :])

        load_x(0)
        for h in range(2):
            wt = keep.tile([P, 4, D], BF16, name="w%d" % h)
            nc.sync.dma_start(out=wt[:], in_=w_view[:, h, :, :])
            for j in range(4):
                w_rows.append(wt[:, j, :])
        for c in range(1, len(LOAD_SLOTS)):
            load_x(c)

        def transpose_pair(rows):
            bank = psum.tile([P, 4 * P], F32, name="tp", tag="bank")
            for a in range(2):
                words = rows[a].bitcast(F32)
                for u in range(2):
                    q = 2 * a + u
                    nc.tensor.transpose(
                        bank[:, q * P : (q + 1) * P], words[:, u::2], ident[:]
                    )
            return bank

        def quantise(grouped, codes, scales):
            nc.vector.quantize_mx(out=codes.bitcast(FP8X4), scales=scales, in_=grouped[:])

        x_grouped = {}
        x_codes = {}
        x_scales = {}

        def gather_x(g):
            bank = transpose_pair(x_rows[2 * g : 2 * g + 2])
            grouped = stage.tile([P, 8 * P], BF16, name="grouped", align_bytes=64)
            nc.scalar.copy(
                out=grouped[:].bitcast(F32).rearrange("p (a c u) -> p a c u", a=2, u=2),
                in_=bank[:].rearrange("p (a u c) -> p a c u", a=2, u=2),
            )
            x_grouped[g] = grouped

        def quantise_x(g):
            x_codes[g] = keep.tile([P, 2 * P], U32, name="xc%d" % g, align_bytes=64)
            x_scales[g] = keep.tile([P, 2 * P], U8, name="xs%d" % g, align_bytes=64)
            quantise(x_grouped[g], x_codes[g][:], x_scales[g][:])

        store_of = {}
        first = 0
        for c, n in enumerate(STORE_SLOTS):
            ot = keep.tile([P, n, E], F32, name="o%d" % c)
            for j in range(n):
                store_of[first + j] = (ot, j, first, n)
            first += n

        w_codes = []
        w_scales = []

        def multiply(g):
            for h in range(2):
                for a in range(2):
                    ot, j, first, n = store_of[2 * g + a]
                    cols = slice(a * P, (a + 1) * P)
                    acc = psum.tile([P, HALF], F32, name="acc", tag="bank")
                    nc.tensor.matmul_mx(
                        out=acc[:],
                        lhsT=x_codes[g][:, cols].bitcast(FP8X4),
                        lhsT_scale=x_scales[g][:, cols],
                        rhs=w_codes[h][:].bitcast(FP8X4),
                        rhs_scale=w_scales[h][:],
                        start=True,
                        stop=True,
                    )
                    dst = ot[:, j, h * HALF : (h + 1) * HALF]
                    if a == 0 or (h == 1 and g % 3 == 2):
                        nc.vector.tensor_copy(out=dst, in_=acc[:])
                    else:
                        nc.scalar.copy(out=dst, in_=acc[:])
            for a in range(2):
                ot, j, first, n = store_of[2 * g + a]
                if j == n - 1:
                    nc.sync.dma_start(out=o_view[:, first : first + n, :], in_=ot[:])

        gather_x(0)
        quantise_x(0)
        for h in range(2):
            wc = keep.tile([P, HALF], U32, name="wc%d" % h, align_bytes=64)
            ws = keep.tile([P, HALF], U8, name="ws%d" % h, align_bytes=64)
            grouped = keep.tile([P, 4 * HALF], BF16, name="wg%d" % h, align_bytes=64)
            words = grouped[:].bitcast(F32).rearrange("p (c b x) -> p b c x", b=2, x=4)
            for b in range(2):
                bank = transpose_pair(w_rows[4 * h + 2 * b : 4 * h + 2 * b + 2])
                copy = nc.scalar.copy if b == 0 else nc.vector.tensor_copy
                copy(out=words[:, b], in_=bank[:].rearrange("p (x c) -> p c x", x=4))
            quantise(grouped, wc[:], ws[:])
            w_codes.append(wc)
            w_scales.append(ws)

        rounds = [[0], [1]] + [[g, g + 1] for g in range(2, PAIRS, 2)] + [[]]
        for k in range(len(rounds) - 1):
            for g in rounds[k + 1]:
                gather_x(g)
            for i, g in enumerate(rounds[k]):
                multiply(g)
                if i == 0:
                    for q in rounds[k + 1]:
                        quantise_x(q)
